import numpy as np
import ml_dtypes


def mxq(x, axis, fmt="e4m3"):
    dtype, down = {"e4m3": (ml_dtypes.float8_e4m3fn, 7), "e5m2": (ml_dtypes.float8_e5m2, 14)}[fmt]
    v = np.moveaxis(np.asarray(x, np.float32).astype(ml_dtypes.bfloat16).astype(np.float64), axis, -1)
    blocks = v.reshape(v.shape[:-1] + (-1, 32))
    amax = np.abs(blocks).max(-1, keepdims=True)
    byte = np.maximum(np.where(amax > 0, np.frexp(amax)[1] - 1 + 127, 0) - down, 1)
    scale = np.exp2(byte - 127.0)
    codes = (blocks / scale).astype(np.float32).astype(dtype).astype(np.float64)
    return np.moveaxis((codes * scale).reshape(v.shape), -1, axis)


WIDE = False


def mx_kscale(k):
    if not WIDE:
        return np.ones(k)
    levels = np.array([10, -10, 5, -5, 0])
    a = np.random.permutation(np.resize(levels, k // 512 * 4)).reshape(k // 512, 4)
    idx = np.arange(k)
    return np.exp2(a[idx // 512, idx % 128 // 32])


BF16 = ml_dtypes.bfloat16


def bf(x):
    return np.asarray(x, np.float32).astype(BF16)


def f64(x):
    return np.asarray(x).astype(np.float64)


N, K, D_IN, HC, H = 1024, 8, 512, 512, 1024


def sigmoid(v):
    return 1.0 / (1.0 + np.exp(-v))


def setup_inputs():
    s, t = mx_kscale(D_IN), mx_kscale(HC)
    return {
        "x": bf(np.random.standard_normal((N, D_IN)) * s),
        "child_h": bf(np.random.standard_normal((N, K, HC)) * t),
        "child_c": bf(np.random.standard_normal((N, K, H)) * 0.5),
        "Wf": bf(np.random.standard_normal((D_IN, H)) * 0.7 / np.sqrt(D_IN) / s[:, None]),
        "bWf": bf(np.random.standard_normal(H) * 0.3),
        "Uf": bf(np.random.standard_normal((HC, H)) * 0.7 / np.sqrt(HC) / t[:, None]),
        "bUf": bf(np.random.standard_normal(H) * 0.3),
    }


def reference(x, child_h, child_c, Wf, bWf, Uf, bUf):
    xf = (mxq(f64(x), 1, "e4m3") @ mxq(f64(Wf), 0, "e4m3")) + f64(bWf)
    hf = mxq(f64(child_h), 2, "e4m3") @ mxq(f64(Uf), 0, "e4m3")
    f = sigmoid(xf[:, None, :] + hf + f64(bUf))
    return (f * f64(child_c)).sum(axis=1)

@@ -1,0 +1,285 @@
+from contextlib import ExitStack
+
+import concourse.mybir as mybir
+from concourse.masks import make_identity
+
+F32 = mybir.dt.float32
+BF16 = mybir.dt.bfloat16
+U32 = mybir.dt.uint32
+U8 = mybir.dt.uint8
+FP8X4 = mybir.dt.float8_e4m3fn_x4
+SIGMOID = mybir.ActivationFunctionType.Sigmoid
+MULT = mybir.AluOpType.mult
+ADD = mybir.AluOpType.add
+
+P = 128
+PACK = 4
+NODES, CHILDREN, FEATURES, HIDDEN = 1024, 8, 512, 1024
+FLOPS = 2 * (NODES * CHILDREN + NODES) * FEATURES * HIDDEN
+
+NODE_BLOCK = 512
+BLOCKS = NODES // NODE_BLOCK
+TILES = NODE_BLOCK // P
+PAIR = 2
+WORDS = FEATURES // PAIR
+HALVES = WORDS // P
+H_BLOCK = PAIR * P
+H_BLOCKS = HIDDEN // H_BLOCK
+STEPS = BLOCKS * CHILDREN
+AHEAD = 3
+
+
+def tile_childsumtreelstmcell_pa_t_kernel(tc, x, child_h, child_c, Wf, bWf, Uf, bUf, out):
+    nc = tc.nc
+    x_view = x.rearrange("(b p t) d -> b p (t d)", b=BLOCKS, t=TILES)
+    h_view = child_h.rearrange("(b p t) k d -> b p t k d", b=BLOCKS, t=TILES)
+    c_view = child_c.rearrange("(b p t) k h -> b p t k h", b=BLOCKS, t=TILES)
+    out_view = out.rearrange("(b p t) h -> b p t h", b=BLOCKS, t=TILES)
+
+    with ExitStack() as ctx:
+        const = ctx.enter_context(tc.tile_pool(name="const", bufs=1))
+        weights = ctx.enter_context(tc.tile_pool(name="weights", bufs=1))
+        wstage = ctx.enter_context(tc.tile_pool(name="wstage", bufs=2))
+        x_rows_pool = ctx.enter_context(tc.tile_pool(name="x_rows", bufs=BLOCKS))
+        h_rows_pool = ctx.enter_context(tc.tile_pool(name="h_rows", bufs=AHEAD))
+        c_rows_pool = ctx.enter_context(tc.tile_pool(name="c_rows", bufs=AHEAD + 1))
+        grouped_pool = ctx.enter_context(tc.tile_pool(name="grouped", bufs=2))
+        codes_pool = ctx.enter_context(tc.tile_pool(name="codes", bufs=2))
+        gate_pool = ctx.enter_context(tc.tile_pool(name="gate", bufs=4))
+        prod_pool = ctx.enter_context(tc.tile_pool(name="prod", bufs=3))
+        sum_pool = ctx.enter_context(tc.tile_pool(name="sums", bufs=2))
+        out_pool = ctx.enter_context(tc.tile_pool(name="out_rows", bufs=2))
+        z_psum = ctx.enter_context(tc.psum_pool(name="z_psum", bufs=3))
+        c_psum = ctx.enter_context(tc.psum_pool(name="c_psum", bufs=3))
+        t_psum = ctx.enter_context(tc.psum_pool(name="t_psum", bufs=2))
+        ctx.enter_context(tc.manual_schedule())
+
+        def load_weight(w):
+            raw = weights.tile([P, PACK * HIDDEN], BF16, name="raw", tag="raw_%s" % w[0])
+            raw_rows = raw[:].rearrange("q (j c) -> q j c", j=PACK)
+            for u in range(HALVES):
+                nc.sync.dma_start(
+                    out=raw_rows[:, PAIR * u : PAIR * (u + 1), :],
+                    in_=w[1][H_BLOCK * u : H_BLOCK * (u + 1), :].rearrange("(q e) c -> q e c", e=PAIR),
+                )
+            return raw
+
+        def regroup_weight_block(raw, hb):
+            grouped_w = wstage.tile([P, H_BLOCK * PACK], BF16, align_bytes=64)
+            nc.vector.tensor_copy(
+                out=grouped_w[:].rearrange("q (e m j) -> q e m j", e=PAIR, j=PACK),
+                in_=raw[:].rearrange("q (j c) -> q j c", j=PACK)[:, :, H_BLOCK * hb : H_BLOCK * (hb + 1)].rearrange(
+                    "q j (m e) -> q e m j", e=PAIR
+                ),
+            )
+            return grouped_w
+
+        def quantise_weight_blocks(hb):
+            cols = slice(H_BLOCK * hb, H_BLOCK * (hb + 1))
+            grouped_u = regroup_weight_block(u_raw, hb)
+            grouped_w = regroup_weight_block(w_raw, hb)
+            nc.vector.quantize_mx(out=u_codes[:, cols].bitcast(FP8X4), scales=u_scales[:, cols], in_=grouped_u[:])
+            nc.vector.quantize_mx(out=w_codes[:, cols].bitcast(FP8X4), scales=w_scales[:, cols], in_=grouped_w[:])
+
+        def load_x(b):
+            rows = x_rows_pool.tile([P, TILES * FEATURES], BF16, name="x_rows")
+            nc.sync.dma_start(out=rows[:], in_=x_view[b])
+            return rows
+
+        def load_children(s):
+            b, k = divmod(s, CHILDREN)
+            rows = h_rows_pool.tile([P, TILES * FEATURES], BF16, name="h_rows")
+            nc.sync.dma_start(out=rows[:].rearrange("p (t d) -> p t d", t=TILES), in_=h_view[b, :, :, k, :])
+            return rows
+
+        def load_cells(s):
+            b, k = divmod(s, CHILDREN)
+            rows = c_rows_pool.tile([P, TILES * HIDDEN], BF16, name="c_rows")
+            nc.sync.dma_start(out=rows[:].rearrange("p (t h) -> p t h", t=TILES), in_=c_view[b, :, :, k, :])
+            return rows
+
+        def transpose_rows(rows):
+            words = rows[:].bitcast(F32)
+            banks = []
+            for half in range(TILES // 2):
+                bank = t_psum.tile([P, 2, HALVES, P], F32, name="bank", tag="t")
+                for a in range(2):
+                    for u in range(HALVES):
+                        first = (2 * half + a) * WORDS + u * P
+                        nc.tensor.transpose(bank[:, a, u, :], words[:, first : first + P], ident[:])
+                banks.append(bank)
+            return banks
+
+        def regroup_rows(banks):
+            grouped = grouped_pool.tile([P, NODE_BLOCK * PACK], BF16, align_bytes=64)
+            grouped_words = grouped[:].bitcast(F32).rearrange("p (h a n u) -> p h a n u", h=2, a=2, u=HALVES)
+            for half in range(TILES // 2):
+                nc.scalar.copy(out=grouped_words[:, half], in_=banks[half][:].rearrange("p a u n -> p a n u"))
+            return grouped
+
+        def quantise_rows(grouped, kind):
+            codes = codes_pool.tile([P, NODE_BLOCK], U32, name="codes", tag="%s_codes" % kind, align_bytes=64)
+            scales = codes_pool.tile([P, NODE_BLOCK], U8, name="scales", tag="%s_scales" % kind, align_bytes=64)
+            nc.vector.quantize_mx(out=codes[:].bitcast(FP8X4), scales=scales[:], in_=grouped[:])
+            return codes, scales
+
+        def gate_sums(hb, e, child, node):
+            z = z_psum.tile([P, NODE_BLOCK], F32)
+            cols = slice((PAIR * hb + e) * P, (PAIR * hb + e + 1) * P)
+            nc.tensor.matmul_mx(
+                out=z[:],
+                lhsT=u_codes[:, cols].bitcast(FP8X4),
+                lhsT_scale=u_scales[:, cols],
+                rhs=child[0][:].bitcast(FP8X4),
+                rhs_scale=child[1][:],
+                start=True,
+                stop=False,
+            )
+            nc.tensor.matmul_mx(
+                out=z[:],
+                lhsT=w_codes[:, cols].bitcast(FP8X4),
+                lhsT_scale=w_scales[:, cols],
+                rhs=node[0][:].bitcast(FP8X4),
+                rhs_scale=node[1][:],
+                start=False,
+                stop=True,
+            )
+            return z
+
+        def transpose_cells(rows, hb):
+            words = rows[:].bitcast(F32)
+            cells = c_psum.tile([P, NODE_BLOCK], F32)
+            for t in range(TILES):
+                first = t * (HIDDEN // PAIR) + hb * P
+                nc.tensor.transpose(cells[:, t * P : (t + 1) * P], words[:, first : first + P], ident[:])
+            return cells
+
+        def store_block(b, hb):
+            total = sums[(b, hb)]
+            rows = out_pool.tile([P, TILES * H_BLOCK], F32, name="out_rows")
+            rows_view = rows[:].rearrange("p (h a w e) -> p h a w e", h=2, a=2, e=PAIR)
+            for half in range(TILES // 2):
+                bank = t_psum.tile([P, 2, PAIR, P], F32, name="bank", tag="t")
+                for a in range(2):
+                    for e in range(PAIR):
+                        first = e * NODE_BLOCK + (2 * half + a) * P
+                        nc.tensor.transpose(bank[:, a, e, :], total[:, first : first + P], ident[:])
+                nc.scalar.copy(out=rows_view[:, half], in_=bank[:].rearrange("p a e w -> p a w e"))
+            nc.sync.dma_start(
+                out=out_view[b, :, :, H_BLOCK * hb : H_BLOCK * (hb + 1)],
+                in_=rows[:].rearrange("p (t h) -> p t h", t=TILES),
+            )
+
+        ident = const.tile([P, P], F32)
+        make_identity(nc, ident[:])
+
+        bias_rows = const.tile([P, P], F32)
+        nc.vector.memset(bias_rows[:], 0.0)
+        bias_rows_bf = bias_rows[:].bitcast(BF16)
+        nc.scalar.dma_start(out=bias_rows_bf[0:H_BLOCKS, :], in_=bWf.rearrange("(r c) -> r c", c=H_BLOCK))
+        nc.scalar.dma_start(out=bias_rows_bf[H_BLOCKS : 2 * H_BLOCKS, :], in_=bUf.rearrange("(r c) -> r c", c=H_BLOCK))
+
+        u_raw = load_weight(("u", Uf))
+        w_raw = load_weight(("w", Wf))
+        h_rows = {0: load_children(0)}
+        x_rows = {0: load_x(0)}
+        c_rows = {0: load_cells(0)}
+        for s in range(1, AHEAD):
+            h_rows[s] = load_children(s)
+            c_rows[s] = load_cells(s)
+        x_rows[1] = load_x(1)
+
+        u_codes = weights.tile([P, HIDDEN], U32, align_bytes=64)
+        u_scales = weights.tile([P, HIDDEN], U8, align_bytes=64)
+        w_codes = weights.tile([P, HIDDEN], U32, align_bytes=64)
+        w_scales = weights.tile([P, HIDDEN], U8, align_bytes=64)
+        for hb in range(0, 2):
+            quantise_weight_blocks(hb)
+
+        bias_ps = t_psum.tile([P, P], F32, name="bias_ps", tag="t")
+        nc.tensor.transpose(bias_ps[:], bias_rows[:], ident[:])
+        both = const.tile([P, 2 * PAIR * H_BLOCKS], F32)
+        nc.vector.tensor_copy(out=both[:], in_=bias_ps[:, 0 : 2 * H_BLOCKS].bitcast(BF16))
+        bias = const.tile([P, PAIR * H_BLOCKS], F32)
+        nc.vector.tensor_tensor(
+            out=bias[:], in0=both[:, 0 : PAIR * H_BLOCKS], in1=both[:, PAIR * H_BLOCKS : 2 * PAIR * H_BLOCKS], op=ADD
+        )
+
+        child = quantise_rows(regroup_rows(transpose_rows(h_rows[0])), "child")
+        node = quantise_rows(regroup_rows(transpose_rows(x_rows[0])), "node")
+        for hb in range(2, H_BLOCKS):
+            quantise_weight_blocks(hb)
+        next_child = None
+        next_node = None
+        sums = {}
+
+        for s in range(STEPS):
+            b, k = divmod(s, CHILDREN)
+            if s + AHEAD < STEPS:
+                h_rows[s + AHEAD] = load_children(s + AHEAD)
+                c_rows[s + AHEAD] = load_cells(s + AHEAD)
+            for first_hb in range(0, H_BLOCKS, 2):
+                pair = (first_hb, first_hb + 1)
+                rows_to_prepare = None
+                if first_hb == 0 and s + 1 < STEPS:
+                    rows_to_prepare = h_rows[s + 1]
+                if first_hb == 2 and k == 0 and b + 1 < BLOCKS:
+                    rows_to_prepare = x_rows[b + 1]
+
+                z = {}
+                for hb in pair:
+                    for e in range(PAIR):
+                        z[(hb, e)] = gate_sums(hb, e, child, node)
+                if rows_to_prepare is not None:
+                    banks = transpose_rows(rows_to_prepare)
+                cells = {}
+                for hb in pair:
+                    cells[hb] = transpose_cells(c_rows[s], hb)
+
+                gates = {}
+                for hb in pair:
+                    gate = gate_pool.tile([P, PAIR * NODE_BLOCK], F32)
+                    for e in range(PAIR):
+                        nc.scalar.activation(
+                            out=gate[:, e * NODE_BLOCK : (e + 1) * NODE_BLOCK],
+                            in_=z[(hb, e)][:],
+                            func=SIGMOID,
+                            bias=bias[:, PAIR * hb + e : PAIR * hb + e + 1],
+                            scale=1.0,
+                        )
+                    gates[hb] = gate
+                if rows_to_prepare is not None:
+                    grouped = regroup_rows(banks)
+
+                for hb in pair:
+                    if k == 0:
+                        total = sum_pool.tile([P, PAIR * NODE_BLOCK], F32, name="total", tag="total%d" % hb)
+                        sums[(b, hb)] = total
+                        product = total
+                    else:
+                        product = prod_pool.tile([P, PAIR * NODE_BLOCK], F32, name="product")
+                    nc.vector.tensor_tensor(
+                        out=product[:].rearrange("p (e n) -> p e n", e=PAIR),
+                        in0=gates[hb][:].rearrange("p (e n) -> p e n", e=PAIR),
+                        in1=cells[hb][:].bitcast(BF16).rearrange("p (n e) -> p e n", e=PAIR),
+                        op=MULT,
+                    )
+                    if hb == pair[0] and rows_to_prepare is not None:
+                        prepared = quantise_rows(grouped, "child" if first_hb == 0 else "node")
+                        if first_hb == 0:
+                            next_child = prepared
+                        else:
+                            next_node = prepared
+                    if k > 0:
+                        adder = nc.gpsimd if hb % 2 == 0 else nc.vector
+                        total = sums[(b, hb)]
+                        adder.tensor_tensor(out=total[:], in0=total[:], in1=product[:], op=ADD)
+
+                if b > 0 and k < H_BLOCKS // 2:
+                    store_block(b - 1, 2 * k + first_hb // 2)
+            child = next_child
+            if k == CHILDREN - 1:
+                node = next_node
+
+        for hb in range(H_BLOCKS):
+            store_block(BLOCKS - 1, hb)

@@ -27,6 +27,8 @@ H_BLOCK = PAIR * P
 H_BLOCKS = HIDDEN // H_BLOCK
 STEPS = BLOCKS * CHILDREN
 AHEAD = 3
+LEAD = 2
+GPSIMD_BLOCKS = 1
 
 
 def tile_childsumtreelstmcell_pa_t_kernel(tc, x, child_h, child_c, Wf, bWf, Uf, bUf, out):
@@ -43,10 +45,10 @@ def tile_childsumtreelstmcell_pa_t_kernel(tc, x, child_h, child_c, Wf, bWf, Uf, 
         x_rows_pool = ctx.enter_context(tc.tile_pool(name="x_rows", bufs=BLOCKS))
         h_rows_pool = ctx.enter_context(tc.tile_pool(name="h_rows", bufs=AHEAD))
         c_rows_pool = ctx.enter_context(tc.tile_pool(name="c_rows", bufs=AHEAD + 1))
-        grouped_pool = ctx.enter_context(tc.tile_pool(name="grouped", bufs=2))
-        codes_pool = ctx.enter_context(tc.tile_pool(name="codes", bufs=2))
-        gate_pool = ctx.enter_context(tc.tile_pool(name="gate", bufs=4))
-        prod_pool = ctx.enter_context(tc.tile_pool(name="prod", bufs=3))
+        grouped_pool = ctx.enter_context(tc.tile_pool(name="grouped", bufs=3))
+        codes_pool = ctx.enter_context(tc.tile_pool(name="codes", bufs=LEAD + 1))
+        gate_pool = ctx.enter_context(tc.tile_pool(name="gate", bufs=6))
+        prod_pool = ctx.enter_context(tc.tile_pool(name="prod", bufs=6))
         sum_pool = ctx.enter_context(tc.tile_pool(name="sums", bufs=2))
         out_pool = ctx.enter_context(tc.tile_pool(name="out_rows", bufs=2))
         z_psum = ctx.enter_context(tc.psum_pool(name="z_psum", bufs=3))
@@ -205,12 +207,11 @@ def tile_childsumtreelstmcell_pa_t_kernel(tc, x, child_h, child_c, Wf, bWf, Uf, 
             out=bias[:], in0=both[:, 0 : PAIR * H_BLOCKS], in1=both[:, PAIR * H_BLOCKS : 2 * PAIR * H_BLOCKS], op=ADD
         )
 
-        child = quantise_rows(regroup_rows(transpose_rows(h_rows[0])), "child")
-        node = quantise_rows(regroup_rows(transpose_rows(x_rows[0])), "node")
+        children = {0: quantise_rows(regroup_rows(transpose_rows(h_rows[0])), "child")}
+        nodes = {0: quantise_rows(regroup_rows(transpose_rows(x_rows[0])), "node")}
         for hb in range(2, H_BLOCKS):
             quantise_weight_blocks(hb)
-        next_child = None
-        next_node = None
+        children[1] = quantise_rows(regroup_rows(transpose_rows(h_rows[1])), "child")
         sums = {}
 
         for s in range(STEPS):
@@ -218,25 +219,26 @@ def tile_childsumtreelstmcell_pa_t_kernel(tc, x, child_h, child_c, Wf, bWf, Uf, 
             if s + AHEAD < STEPS:
                 h_rows[s + AHEAD] = load_children(s + AHEAD)
                 c_rows[s + AHEAD] = load_cells(s + AHEAD)
+            gates = {}
+            cells = {}
+            grouped = {}
             for first_hb in range(0, H_BLOCKS, 2):
                 pair = (first_hb, first_hb + 1)
                 rows_to_prepare = None
-                if first_hb == 0 and s + 1 < STEPS:
-                    rows_to_prepare = h_rows[s + 1]
+                if first_hb == 0 and s + LEAD < STEPS:
+                    rows_to_prepare = h_rows[s + LEAD]
                 if first_hb == 2 and k == 0 and b + 1 < BLOCKS:
                     rows_to_prepare = x_rows[b + 1]
 
                 z = {}
                 for hb in pair:
                     for e in range(PAIR):
-                        z[(hb, e)] = gate_sums(hb, e, child, node)
+                        z[(hb, e)] = gate_sums(hb, e, children[s], nodes[b])
                 if rows_to_prepare is not None:
                     banks = transpose_rows(rows_to_prepare)
-                cells = {}
                 for hb in pair:
                     cells[hb] = transpose_cells(c_rows[s], hb)
 
-                gates = {}
                 for hb in pair:
                     gate = gate_pool.tile([P, PAIR * NODE_BLOCK], F32)
                     for e in range(PAIR):
@@ -249,37 +251,37 @@ def tile_childsumtreelstmcell_pa_t_kernel(tc, x, child_h, child_c, Wf, bWf, Uf, 
                         )
                     gates[hb] = gate
                 if rows_to_prepare is not None:
-                    grouped = regroup_rows(banks)
-
-                for hb in pair:
-                    if k == 0:
-                        total = sum_pool.tile([P, PAIR * NODE_BLOCK], F32, name="total", tag="total%d" % hb)
-                        sums[(b, hb)] = total
-                        product = total
-                    else:
-                        product = prod_pool.tile([P, PAIR * NODE_BLOCK], F32, name="product")
-                    nc.vector.tensor_tensor(
-                        out=product[:].rearrange("p (e n) -> p e n", e=PAIR),
-                        in0=gates[hb][:].rearrange("p (e n) -> p e n", e=PAIR),
-                        in1=cells[hb][:].bitcast(BF16).rearrange("p (n e) -> p e n", e=PAIR),
-                        op=MULT,
-                    )
-                    if hb == pair[0] and rows_to_prepare is not None:
-                        prepared = quantise_rows(grouped, "child" if first_hb == 0 else "node")
-                        if first_hb == 0:
-                            next_child = prepared
-                        else:
-                            next_node = prepared
-                    if k > 0:
-                        adder = nc.gpsimd if hb % 2 == 0 else nc.vector
-                        total = sums[(b, hb)]
-                        adder.tensor_tensor(out=total[:], in0=total[:], in1=product[:], op=ADD)
+                    grouped[first_hb] = regroup_rows(banks)
 
                 if b > 0 and k < H_BLOCKS // 2:
                     store_block(b - 1, 2 * k + first_hb // 2)
-            child = next_child
-            if k == CHILDREN - 1:
-                node = next_node
+
+            products = {}
+            for hb in range(H_BLOCKS):
+                if k == 0:
+                    total = sum_pool.tile([P, PAIR * NODE_BLOCK], F32, name="total", tag="total%d" % hb)
+                    sums[(b, hb)] = total
+                    products[hb] = total
+                else:
+                    product = prod_pool.tile([P, PAIR * NODE_BLOCK], F32)
+                    products[hb] = product
+                nc.vector.tensor_tensor(
+                    out=products[hb][:].rearrange("p (e n) -> p e n", e=PAIR),
+                    in0=gates[hb][:].rearrange("p (e n) -> p e n", e=PAIR),
+                    in1=cells[hb][:].bitcast(BF16).rearrange("p (n e) -> p e n", e=PAIR),
+                    op=MULT,
+                )
+                if k > 0 and hb < GPSIMD_BLOCKS:
+                    total = sums[(b, hb)]
+                    nc.gpsimd.tensor_tensor(out=total[:], in0=total[:], in1=products[hb][:], op=ADD)
+            if k > 0:
+                for hb in range(GPSIMD_BLOCKS, H_BLOCKS):
+                    total = sums[(b, hb)]
+                    nc.vector.tensor_tensor(out=total[:], in0=total[:], in1=products[hb][:], op=ADD)
+            if 0 in grouped:
+                children[s + LEAD] = quantise_rows(grouped[0], "child")
+            if 2 in grouped:
+                nodes[b + 1] = quantise_rows(grouped[2], "node")
 
         for hb in range(H_BLOCKS):
             store_block(BLOCKS - 1, hb)

@@ -28,7 +28,9 @@ H_BLOCKS = HIDDEN // H_BLOCK
 STEPS = BLOCKS * CHILDREN
 AHEAD = 3
 LEAD = 2
-GPSIMD_BLOCKS = 1
+BLOCK_COLUMNS = PAIR * NODE_BLOCK
+STEP_COLUMNS = H_BLOCKS * BLOCK_COLUMNS
+GPSIMD_COLUMNS = 3 * NODE_BLOCK
 
 
 def tile_childsumtreelstmcell_pa_t_kernel(tc, x, child_h, child_c, Wf, bWf, Uf, bUf, out):
@@ -48,7 +50,7 @@ def tile_childsumtreelstmcell_pa_t_kernel(tc, x, child_h, child_c, Wf, bWf, Uf, 
         grouped_pool = ctx.enter_context(tc.tile_pool(name="grouped", bufs=3))
         codes_pool = ctx.enter_context(tc.tile_pool(name="codes", bufs=LEAD + 1))
         gate_pool = ctx.enter_context(tc.tile_pool(name="gate", bufs=6))
-        prod_pool = ctx.enter_context(tc.tile_pool(name="prod", bufs=6))
+        prod_pool = ctx.enter_context(tc.tile_pool(name="prod", bufs=2))
         sum_pool = ctx.enter_context(tc.tile_pool(name="sums", bufs=2))
         out_pool = ctx.enter_context(tc.tile_pool(name="out_rows", bufs=2))
         z_psum = ctx.enter_context(tc.psum_pool(name="z_psum", bufs=3))
@@ -157,7 +159,7 @@ def tile_childsumtreelstmcell_pa_t_kernel(tc, x, child_h, child_c, Wf, bWf, Uf, 
             return cells
 
         def store_block(b, hb):
-            total = sums[(b, hb)]
+            total = sums[b][:, hb * BLOCK_COLUMNS : (hb + 1) * BLOCK_COLUMNS]
             rows = out_pool.tile([P, TILES * H_BLOCK], F32, name="out_rows")
             rows_view = rows[:].rearrange("p (h a w e) -> p h a w e", h=2, a=2, e=PAIR)
             for half in range(TILES // 2):
@@ -256,28 +258,34 @@ def tile_childsumtreelstmcell_pa_t_kernel(tc, x, child_h, child_c, Wf, bWf, Uf, 
                 if b > 0 and k < H_BLOCKS // 2:
                     store_block(b - 1, 2 * k + first_hb // 2)
 
-            products = {}
+            if k == 0:
+                sums[b] = sum_pool.tile([P, STEP_COLUMNS], F32, name="total")
+                products = sums[b]
+            else:
+                products = prod_pool.tile([P, STEP_COLUMNS], F32, name="products")
+            total = sums[b]
             for hb in range(H_BLOCKS):
-                if k == 0:
-                    total = sum_pool.tile([P, PAIR * NODE_BLOCK], F32, name="total", tag="total%d" % hb)
-                    sums[(b, hb)] = total
-                    products[hb] = total
-                else:
-                    product = prod_pool.tile([P, PAIR * NODE_BLOCK], F32)
-                    products[hb] = product
+                first, last = hb * BLOCK_COLUMNS, (hb + 1) * BLOCK_COLUMNS
                 nc.vector.tensor_tensor(
-                    out=products[hb][:].rearrange("p (e n) -> p e n", e=PAIR),
+                    out=products[:, first:last].rearrange("p (e n) -> p e n", e=PAIR),
                     in0=gates[hb][:].rearrange("p (e n) -> p e n", e=PAIR),
                     in1=cells[hb][:].bitcast(BF16).rearrange("p (n e) -> p e n", e=PAIR),
                     op=MULT,
                 )
-                if k > 0 and hb < GPSIMD_BLOCKS:
-                    total = sums[(b, hb)]
-                    nc.gpsimd.tensor_tensor(out=total[:], in0=total[:], in1=products[hb][:], op=ADD)
-            if k > 0:
-                for hb in range(GPSIMD_BLOCKS, H_BLOCKS):
-                    total = sums[(b, hb)]
-                    nc.vector.tensor_tensor(out=total[:], in0=total[:], in1=products[hb][:], op=ADD)
+                last = min(last, GPSIMD_COLUMNS)
+                if k > 0 and first < last:
+                    nc.gpsimd.tensor_tensor(
+                        out=total[:, first:last], in0=total[:, first:last], in1=products[:, first:last], op=ADD
+                    )
+            if k == CHILDREN - 1:
+                bounds = [max(hb * BLOCK_COLUMNS, GPSIMD_COLUMNS) for hb in range(H_BLOCKS)] + [STEP_COLUMNS]
+            else:
+                bounds = [GPSIMD_COLUMNS, STEP_COLUMNS]
+            for first, last in zip(bounds[:-1], bounds[1:]):
+                if k > 0 and first < last:
+                    nc.vector.tensor_tensor(
+                        out=total[:, first:last], in0=total[:, first:last], in1=products[:, first:last], op=ADD
+                    )
             if 0 in grouped:
                 children[s + LEAD] = quantise_rows(grouped[0], "child")
             if 2 in grouped:

@@ -25,12 +25,15 @@ WORDS = FEATURES // PAIR
 HALVES = WORDS // P
 H_BLOCK = PAIR * P
 H_BLOCKS = HIDDEN // H_BLOCK
+W_PARTS = 2
+W_PART = HIDDEN // W_PARTS
 STEPS = BLOCKS * CHILDREN
 AHEAD = 3
 LEAD = 2
+X_STEP = 2
 BLOCK_COLUMNS = PAIR * NODE_BLOCK
 STEP_COLUMNS = H_BLOCKS * BLOCK_COLUMNS
-GPSIMD_COLUMNS = 3 * NODE_BLOCK
+GPSIMD_COLUMNS = BLOCK_COLUMNS
 
 
 def tile_childsumtreelstmcell_pa_t_kernel(tc, x, child_h, child_c, Wf, bWf, Uf, bUf, out):
@@ -52,27 +55,30 @@ def tile_childsumtreelstmcell_pa_t_kernel(tc, x, child_h, child_c, Wf, bWf, Uf, 
         gate_pool = ctx.enter_context(tc.tile_pool(name="gate", bufs=6))
         prod_pool = ctx.enter_context(tc.tile_pool(name="prod", bufs=2))
         sum_pool = ctx.enter_context(tc.tile_pool(name="sums", bufs=2))
-        out_pool = ctx.enter_context(tc.tile_pool(name="out_rows", bufs=2))
+        out_pool = ctx.enter_context(tc.tile_pool(name="out_rows", bufs=H_BLOCKS))
         z_psum = ctx.enter_context(tc.psum_pool(name="z_psum", bufs=3))
         c_psum = ctx.enter_context(tc.psum_pool(name="c_psum", bufs=3))
         t_psum = ctx.enter_context(tc.psum_pool(name="t_psum", bufs=2))
         ctx.enter_context(tc.manual_schedule())
 
-        def load_weight(w):
-            raw = weights.tile([P, PACK * HIDDEN], BF16, name="raw", tag="raw_%s" % w[0])
+        def load_weight_part(w, name, part):
+            raw = weights.tile([P, PACK * W_PART], BF16, name="raw", tag="raw_%s%d" % (name, part))
             raw_rows = raw[:].rearrange("q (j c) -> q j c", j=PACK)
             for u in range(HALVES):
                 nc.sync.dma_start(
                     out=raw_rows[:, PAIR * u : PAIR * (u + 1), :],
-                    in_=w[1][H_BLOCK * u : H_BLOCK * (u + 1), :].rearrange("(q e) c -> q e c", e=PAIR),
+                    in_=w[PAIR * P * u : PAIR * P * (u + 1), W_PART * part : W_PART * (part + 1)].rearrange(
+                        "(q e) c -> q e c", e=PAIR
+                    ),
                 )
             return raw
 
-        def regroup_weight_block(raw, hb):
+        def regroup_weight_block(raw_parts, hb):
+            part, first = divmod(H_BLOCK * hb, W_PART)
             grouped_w = wstage.tile([P, H_BLOCK * PACK], BF16, align_bytes=64)
             nc.vector.tensor_copy(
                 out=grouped_w[:].rearrange("q (e m j) -> q e m j", e=PAIR, j=PACK),
-                in_=raw[:].rearrange("q (j c) -> q j c", j=PACK)[:, :, H_BLOCK * hb : H_BLOCK * (hb + 1)].rearrange(
+                in_=raw_parts[part][:].rearrange("q (j c) -> q j c", j=PACK)[:, :, first : first + H_BLOCK].rearrange(
                     "q j (m e) -> q e m j", e=PAIR
                 ),
             )
@@ -183,21 +189,24 @@ def tile_childsumtreelstmcell_pa_t_kernel(tc, x, child_h, child_c, Wf, bWf, Uf, 
         nc.scalar.dma_start(out=bias_rows_bf[0:H_BLOCKS, :], in_=bWf.rearrange("(r c) -> r c", c=H_BLOCK))
         nc.scalar.dma_start(out=bias_rows_bf[H_BLOCKS : 2 * H_BLOCKS, :], in_=bUf.rearrange("(r c) -> r c", c=H_BLOCK))
 
-        u_raw = load_weight(("u", Uf))
-        w_raw = load_weight(("w", Wf))
+        u_raw = {0: load_weight_part(Uf, "u", 0)}
+        w_raw = {0: load_weight_part(Wf, "w", 0)}
         h_rows = {0: load_children(0)}
         x_rows = {0: load_x(0)}
+        h_rows[1] = load_children(1)
+        u_raw[1] = load_weight_part(Uf, "u", 1)
+        w_raw[1] = load_weight_part(Wf, "w", 1)
         c_rows = {0: load_cells(0)}
-        for s in range(1, AHEAD):
-            h_rows[s] = load_children(s)
-            c_rows[s] = load_cells(s)
+        h_rows[2] = load_children(2)
+        c_rows[1] = load_cells(1)
+        c_rows[2] = load_cells(2)
         x_rows[1] = load_x(1)
 
         u_codes = weights.tile([P, HIDDEN], U32, align_bytes=64)
         u_scales = weights.tile([P, HIDDEN], U8, align_bytes=64)
         w_codes = weights.tile([P, HIDDEN], U32, align_bytes=64)
         w_scales = weights.tile([P, HIDDEN], U8, align_bytes=64)
-        for hb in range(0, 2):
+        for hb in range(0, H_BLOCKS // W_PARTS):
             quantise_weight_blocks(hb)
 
         bias_ps = t_psum.tile([P, P], F32, name="bias_ps", tag="t")
@@ -211,9 +220,10 @@ def tile_childsumtreelstmcell_pa_t_kernel(tc, x, child_h, child_c, Wf, bWf, Uf, 
 
         children = {0: quantise_rows(regroup_rows(transpose_rows(h_rows[0])), "child")}
         nodes = {0: quantise_rows(regroup_rows(transpose_rows(x_rows[0])), "node")}
-        for hb in range(2, H_BLOCKS):
+        grouped_1 = regroup_rows(transpose_rows(h_rows[1]))
+        for hb in range(H_BLOCKS // W_PARTS, H_BLOCKS):
             quantise_weight_blocks(hb)
-        children[1] = quantise_rows(regroup_rows(transpose_rows(h_rows[1])), "child")
+        children[1] = quantise_rows(grouped_1, "child")
         sums = {}
 
         for s in range(STEPS):
@@ -227,10 +237,10 @@ def tile_childsumtreelstmcell_pa_t_kernel(tc, x, child_h, child_c, Wf, bWf, Uf, 
             for first_hb in range(0, H_BLOCKS, 2):
                 pair = (first_hb, first_hb + 1)
                 rows_to_prepare = None
-                if first_hb == 0 and s + LEAD < STEPS:
-                    rows_to_prepare = h_rows[s + LEAD]
-                if first_hb == 2 and k == 0 and b + 1 < BLOCKS:
+                if first_hb == 0 and k == X_STEP and b + 1 < BLOCKS:
                     rows_to_prepare = x_rows[b + 1]
+                if first_hb == 2 and s + LEAD < STEPS:
+                    rows_to_prepare = h_rows[s + LEAD]
 
                 z = {}
                 for hb in pair:
@@ -242,7 +252,7 @@ def tile_childsumtreelstmcell_pa_t_kernel(tc, x, child_h, child_c, Wf, bWf, Uf, 
                     cells[hb] = transpose_cells(c_rows[s], hb)
 
                 for hb in pair:
-                    gate = gate_pool.tile([P, PAIR * NODE_BLOCK], F32)
+                    gate = gate_pool.tile([P, BLOCK_COLUMNS], F32)
                     for e in range(PAIR):
                         nc.scalar.activation(
                             out=gate[:, e * NODE_BLOCK : (e + 1) * NODE_BLOCK],
@@ -255,8 +265,8 @@ def tile_childsumtreelstmcell_pa_t_kernel(tc, x, child_h, child_c, Wf, bWf, Uf, 
                 if rows_to_prepare is not None:
                     grouped[first_hb] = regroup_rows(banks)
 
-                if b > 0 and k < H_BLOCKS // 2:
-                    store_block(b - 1, 2 * k + first_hb // 2)
+                if b > 0 and 1 <= k <= H_BLOCKS // 2:
+                    store_block(b - 1, 2 * (k - 1) + first_hb // 2)
 
             if k == 0:
                 sums[b] = sum_pool.tile([P, STEP_COLUMNS], F32, name="total")
@@ -277,6 +287,10 @@ def tile_childsumtreelstmcell_pa_t_kernel(tc, x, child_h, child_c, Wf, bWf, Uf, 
                     nc.gpsimd.tensor_tensor(
                         out=total[:, first:last], in0=total[:, first:last], in1=products[:, first:last], op=ADD
                     )
+            if 0 in grouped:
+                nodes[b + 1] = quantise_rows(grouped[0], "node")
+            if 2 in grouped:
+                children[s + LEAD] = quantise_rows(grouped[2], "child")
             if k == CHILDREN - 1:
                 bounds = [max(hb * BLOCK_COLUMNS, GPSIMD_COLUMNS) for hb in range(H_BLOCKS)] + [STEP_COLUMNS]
             else:
@@ -286,10 +300,6 @@ def tile_childsumtreelstmcell_pa_t_kernel(tc, x, child_h, child_c, Wf, bWf, Uf, 
                     nc.vector.tensor_tensor(
                         out=total[:, first:last], in0=total[:, first:last], in1=products[:, first:last], op=ADD
                     )
-            if 0 in grouped:
-                children[s + LEAD] = quantise_rows(grouped[0], "child")
-            if 2 in grouped:
-                nodes[b + 1] = quantise_rows(grouped[2], "node")
 
         for hb in range(H_BLOCKS):
             store_block(BLOCKS - 1, hb)

from contextlib import ExitStack

import concourse.mybir as mybir
from concourse.masks import make_identity

F32 = mybir.dt.float32
BF16 = mybir.dt.bfloat16
U32 = mybir.dt.uint32
U8 = mybir.dt.uint8
FP8X4 = mybir.dt.float8_e4m3fn_x4
SIGMOID = mybir.ActivationFunctionType.Sigmoid
MULT = mybir.AluOpType.mult
ADD = mybir.AluOpType.add

P = 128
PACK = 4
NODES, CHILDREN, FEATURES, HIDDEN = 1024, 8, 512, 1024
FLOPS = 2 * (NODES * CHILDREN + NODES) * FEATURES * HIDDEN

NODE_BLOCK = 512
BLOCKS = NODES // NODE_BLOCK
TILES = NODE_BLOCK // P
PAIR = 2
WORDS = FEATURES // PAIR
HALVES = WORDS // P
H_BLOCK = PAIR * P
H_BLOCKS = HIDDEN // H_BLOCK
W_PARTS = 2
W_PART = HIDDEN // W_PARTS
STEPS = BLOCKS * CHILDREN
AHEAD = 3
LEAD = 2
X_STEP = 2
BLOCK_COLUMNS = PAIR * NODE_BLOCK
STEP_COLUMNS = H_BLOCKS * BLOCK_COLUMNS
GPSIMD_COLUMNS = BLOCK_COLUMNS


def tile_childsumtreelstmcell_pa_t_kernel(tc, x, child_h, child_c, Wf, bWf, Uf, bUf, out):
    nc = tc.nc
    x_view = x.rearrange("(b p t) d -> b p (t d)", b=BLOCKS, t=TILES)
    h_view = child_h.rearrange("(b p t) k d -> b p t k d", b=BLOCKS, t=TILES)
    c_view = child_c.rearrange("(b p t) k h -> b p t k h", b=BLOCKS, t=TILES)
    out_view = out.rearrange("(b p t) h -> b p t h", b=BLOCKS, t=TILES)

    with ExitStack() as ctx:
        const = ctx.enter_context(tc.tile_pool(name="const", bufs=1))
        weights = ctx.enter_context(tc.tile_pool(name="weights", bufs=1))
        wstage = ctx.enter_context(tc.tile_pool(name="wstage", bufs=2))
        x_rows_pool = ctx.enter_context(tc.tile_pool(name="x_rows", bufs=BLOCKS))
        h_rows_pool = ctx.enter_context(tc.tile_pool(name="h_rows", bufs=AHEAD))
        c_rows_pool = ctx.enter_context(tc.tile_pool(name="c_rows", bufs=AHEAD + 1))
        grouped_pool = ctx.enter_context(tc.tile_pool(name="grouped", bufs=3))
        codes_pool = ctx.enter_context(tc.tile_pool(name="codes", bufs=LEAD + 1))
        gate_pool = ctx.enter_context(tc.tile_pool(name="gate", bufs=6))
        prod_pool = ctx.enter_context(tc.tile_pool(name="prod", bufs=2))
        sum_pool = ctx.enter_context(tc.tile_pool(name="sums", bufs=2))
        out_pool = ctx.enter_context(tc.tile_pool(name="out_rows", bufs=H_BLOCKS))
        z_psum = ctx.enter_context(tc.psum_pool(name="z_psum", bufs=3))
        c_psum = ctx.enter_context(tc.psum_pool(name="c_psum", bufs=3))
        t_psum = ctx.enter_context(tc.psum_pool(name="t_psum", bufs=2))
        ctx.enter_context(tc.manual_schedule())

        def load_weight_part(w, name, part):
            raw = weights.tile([P, PACK * W_PART], BF16, name="raw", tag="raw_%s%d" % (name, part))
            raw_rows = raw[:].rearrange("q (j c) -> q j c", j=PACK)
            for u in range(HALVES):
                nc.sync.dma_start(
                    out=raw_rows[:, PAIR * u : PAIR * (u + 1), :],
                    in_=w[PAIR * P * u : PAIR * P * (u + 1), W_PART * part : W_PART * (part + 1)].rearrange(
                        "(q e) c -> q e c", e=PAIR
                    ),
                )
            return raw

        def regroup_weight_block(raw_parts, hb):
            part, first = divmod(H_BLOCK * hb, W_PART)
            grouped_w = wstage.tile([P, H_BLOCK * PACK], BF16, align_bytes=64)
            nc.vector.tensor_copy(
                out=grouped_w[:].rearrange("q (e m j) -> q e m j", e=PAIR, j=PACK),
                in_=raw_parts[part][:].rearrange("q (j c) -> q j c", j=PACK)[:, :, first : first + H_BLOCK].rearrange(
                    "q j (m e) -> q e m j", e=PAIR
                ),
            )
            return grouped_w

        def quantise_weight_blocks(hb):
            cols = slice(H_BLOCK * hb, H_BLOCK * (hb + 1))
            grouped_u = regroup_weight_block(u_raw, hb)
            grouped_w = regroup_weight_block(w_raw, hb)
            nc.vector.quantize_mx(out=u_codes[:, cols].bitcast(FP8X4), scales=u_scales[:, cols], in_=grouped_u[:])
            nc.vector.quantize_mx(out=w_codes[:, cols].bitcast(FP8X4), scales=w_scales[:, cols], in_=grouped_w[:])

        def load_x(b):
            rows = x_rows_pool.tile([P, TILES * FEATURES], BF16, name="x_rows")
            nc.sync.dma_start(out=rows[:], in_=x_view[b])
            return rows

        def load_children(s):
            b, k = divmod(s, CHILDREN)
            rows = h_rows_pool.tile([P, TILES * FEATURES], BF16, name="h_rows")
            nc.sync.dma_start(out=rows[:].rearrange("p (t d) -> p t d", t=TILES), in_=h_view[b, :, :, k, :])
            return rows

        def load_cells(s):
            b, k = divmod(s, CHILDREN)
            rows = c_rows_pool.tile([P, TILES * HIDDEN], BF16, name="c_rows")
            nc.sync.dma_start(out=rows[:].rearrange("p (t h) -> p t h", t=TILES), in_=c_view[b, :, :, k, :])
            return rows

        def transpose_rows(rows):
            words = rows[:].bitcast(F32)
            banks = []
            for half in range(TILES // 2):
                bank = t_psum.tile([P, 2, HALVES, P], F32, name="bank", tag="t")
                for a in range(2):
                    for u in range(HALVES):
                        first = (2 * half + a) * WORDS + u * P
                        nc.tensor.transpose(bank[:, a, u, :], words[:, first : first + P], ident[:])
                banks.append(bank)
            return banks

        def regroup_rows(banks):
            grouped = grouped_pool.tile([P, NODE_BLOCK * PACK], BF16, align_bytes=64)
            grouped_words = grouped[:].bitcast(F32).rearrange("p (h a n u) -> p h a n u", h=2, a=2, u=HALVES)
            for half in range(TILES // 2):
                nc.scalar.copy(out=grouped_words[:, half], in_=banks[half][:].rearrange("p a u n -> p a n u"))
            return grouped

        def quantise_rows(grouped, kind):
            codes = codes_pool.tile([P, NODE_BLOCK], U32, name="codes", tag="%s_codes" % kind, align_bytes=64)
            scales = codes_pool.tile([P, NODE_BLOCK], U8, name="scales", tag="%s_scales" % kind, align_bytes=64)
            nc.vector.quantize_mx(out=codes[:].bitcast(FP8X4), scales=scales[:], in_=grouped[:])
            return codes, scales

        def gate_sums(hb, e, child, node):
            z = z_psum.tile([P, NODE_BLOCK], F32)
            cols = slice((PAIR * hb + e) * P, (PAIR * hb + e + 1) * P)
            nc.tensor.matmul_mx(
                out=z[:],
                lhsT=u_codes[:, cols].bitcast(FP8X4),
                lhsT_scale=u_scales[:, cols],
                rhs=child[0][:].bitcast(FP8X4),
                rhs_scale=child[1][:],
                start=True,
                stop=False,
            )
            nc.tensor.matmul_mx(
                out=z[:],
                lhsT=w_codes[:, cols].bitcast(FP8X4),
                lhsT_scale=w_scales[:, cols],
                rhs=node[0][:].bitcast(FP8X4),
                rhs_scale=node[1][:],
                start=False,
                stop=True,
            )
            return z

        def transpose_cells(rows, hb):
            words = rows[:].bitcast(F32)
            cells = c_psum.tile([P, NODE_BLOCK], F32)
            for t in range(TILES):
                first = t * (HIDDEN // PAIR) + hb * P
                nc.tensor.transpose(cells[:, t * P : (t + 1) * P], words[:, first : first + P], ident[:])
            return cells

        def store_block(b, hb):
            total = sums[b][:, hb * BLOCK_COLUMNS : (hb + 1) * BLOCK_COLUMNS]
            rows = out_pool.tile([P, TILES * H_BLOCK], F32, name="out_rows")
            rows_view = rows[:].rearrange("p (h a w e) -> p h a w e", h=2, a=2, e=PAIR)
            for half in range(TILES // 2):
                bank = t_psum.tile([P, 2, PAIR, P], F32, name="bank", tag="t")
                for a in range(2):
                    for e in range(PAIR):
                        first = e * NODE_BLOCK + (2 * half + a) * P
                        nc.tensor.transpose(bank[:, a, e, :], total[:, first : first + P], ident[:])
                nc.scalar.copy(out=rows_view[:, half], in_=bank[:].rearrange("p a e w -> p a w e"))
            nc.sync.dma_start(
                out=out_view[b, :, :, H_BLOCK * hb : H_BLOCK * (hb + 1)],
                in_=rows[:].rearrange("p (t h) -> p t h", t=TILES),
            )

        ident = const.tile([P, P], F32)
        make_identity(nc, ident[:])

        bias_rows = const.tile([P, P], F32)
        nc.vector.memset(bias_rows[:], 0.0)
        bias_rows_bf = bias_rows[:].bitcast(BF16)
        nc.scalar.dma_start(out=bias_rows_bf[0:H_BLOCKS, :], in_=bWf.rearrange("(r c) -> r c", c=H_BLOCK))
        nc.scalar.dma_start(out=bias_rows_bf[H_BLOCKS : 2 * H_BLOCKS, :], in_=bUf.rearrange("(r c) -> r c", c=H_BLOCK))

        u_raw = {0: load_weight_part(Uf, "u", 0)}
        w_raw = {0: load_weight_part(Wf, "w", 0)}
        h_rows = {0: load_children(0)}
        x_rows = {0: load_x(0)}
        h_rows[1] = load_children(1)
        u_raw[1] = load_weight_part(Uf, "u", 1)
        w_raw[1] = load_weight_part(Wf, "w", 1)
        c_rows = {0: load_cells(0)}
        h_rows[2] = load_children(2)
        c_rows[1] = load_cells(1)
        c_rows[2] = load_cells(2)
        x_rows[1] = load_x(1)

        u_codes = weights.tile([P, HIDDEN], U32, align_bytes=64)
        u_scales = weights.tile([P, HIDDEN], U8, align_bytes=64)
        w_codes = weights.tile([P, HIDDEN], U32, align_bytes=64)
        w_scales = weights.tile([P, HIDDEN], U8, align_bytes=64)
        for hb in range(0, H_BLOCKS // W_PARTS):
            quantise_weight_blocks(hb)

        bias_ps = t_psum.tile([P, P], F32, name="bias_ps", tag="t")
        nc.tensor.transpose(bias_ps[:], bias_rows[:], ident[:])
        both = const.tile([P, 2 * PAIR * H_BLOCKS], F32)
        nc.vector.tensor_copy(out=both[:], in_=bias_ps[:, 0 : 2 * H_BLOCKS].bitcast(BF16))
        bias = const.tile([P, PAIR * H_BLOCKS], F32)
        nc.vector.tensor_tensor(
            out=bias[:], in0=both[:, 0 : PAIR * H_BLOCKS], in1=both[:, PAIR * H_BLOCKS : 2 * PAIR * H_BLOCKS], op=ADD
        )

        children = {0: quantise_rows(regroup_rows(transpose_rows(h_rows[0])), "child")}
        nodes = {0: quantise_rows(regroup_rows(transpose_rows(x_rows[0])), "node")}
        grouped_1 = regroup_rows(transpose_rows(h_rows[1]))
        for hb in range(H_BLOCKS // W_PARTS, H_BLOCKS):
            quantise_weight_blocks(hb)
        children[1] = quantise_rows(grouped_1, "child")
        sums = {}

        for s in range(STEPS):
            b, k = divmod(s, CHILDREN)
            if s + AHEAD < STEPS:
                h_rows[s + AHEAD] = load_children(s + AHEAD)
                c_rows[s + AHEAD] = load_cells(s + AHEAD)
            gates = {}
            cells = {}
            grouped = {}
            for first_hb in range(0, H_BLOCKS, 2):
                pair = (first_hb, first_hb + 1)
                rows_to_prepare = None
                if first_hb == 0 and k == X_STEP and b + 1 < BLOCKS:
                    rows_to_prepare = x_rows[b + 1]
                if first_hb == 2 and s + LEAD < STEPS:
                    rows_to_prepare = h_rows[s + LEAD]

                z = {}
                for hb in pair:
                    for e in range(PAIR):
                        z[(hb, e)] = gate_sums(hb, e, children[s], nodes[b])
                if rows_to_prepare is not None:
                    banks = transpose_rows(rows_to_prepare)
                for hb in pair:
                    cells[hb] = transpose_cells(c_rows[s], hb)

                for hb in pair:
                    gate = gate_pool.tile([P, BLOCK_COLUMNS], F32)
                    for e in range(PAIR):
                        nc.scalar.activation(
                            out=gate[:, e * NODE_BLOCK : (e + 1) * NODE_BLOCK],
                            in_=z[(hb, e)][:],
                            func=SIGMOID,
                            bias=bias[:, PAIR * hb + e : PAIR * hb + e + 1],
                            scale=1.0,
                        )
                    gates[hb] = gate
                if rows_to_prepare is not None:
                    grouped[first_hb] = regroup_rows(banks)

                if b > 0 and 1 <= k <= H_BLOCKS // 2:
                    store_block(b - 1, 2 * (k - 1) + first_hb // 2)

            if k == 0:
                sums[b] = sum_pool.tile([P, STEP_COLUMNS], F32, name="total")
                products = sums[b]
            else:
                products = prod_pool.tile([P, STEP_COLUMNS], F32, name="products")
            total = sums[b]
            for hb in range(H_BLOCKS):
                first, last = hb * BLOCK_COLUMNS, (hb + 1) * BLOCK_COLUMNS
                nc.vector.tensor_tensor(
                    out=products[:, first:last].rearrange("p (e n) -> p e n", e=PAIR),
                    in0=gates[hb][:].rearrange("p (e n) -> p e n", e=PAIR),
                    in1=cells[hb][:].bitcast(BF16).rearrange("p (n e) -> p e n", e=PAIR),
                    op=MULT,
                )
                last = min(last, GPSIMD_COLUMNS)
                if k > 0 and first < last:
                    nc.gpsimd.tensor_tensor(
                        out=total[:, first:last], in0=total[:, first:last], in1=products[:, first:last], op=ADD
                    )
            if 0 in grouped:
                nodes[b + 1] = quantise_rows(grouped[0], "node")
            if 2 in grouped:
                children[s + LEAD] = quantise_rows(grouped[2], "child")
            if k == CHILDREN - 1:
                bounds = [max(hb * BLOCK_COLUMNS, GPSIMD_COLUMNS) for hb in range(H_BLOCKS)] + [STEP_COLUMNS]
            else:
                bounds = [GPSIMD_COLUMNS, STEP_COLUMNS]
            for first, last in zip(bounds[:-1], bounds[1:]):
                if k > 0 and first < last:
                    nc.vector.tensor_tensor(
                        out=total[:, first:last], in0=total[:, first:last], in1=products[:, first:last], op=ADD
                    )

        for hb in range(H_BLOCKS):
            store_block(BLOCKS - 1, hb)
